import numpy as np
import ml_dtypes


def mxq(x, axis, fmt="e4m3"):
    dtype, down = {"e4m3": (ml_dtypes.float8_e4m3fn, 7), "e5m2": (ml_dtypes.float8_e5m2, 14)}[fmt]
    v = np.moveaxis(np.asarray(x, np.float32).astype(ml_dtypes.bfloat16).astype(np.float64), axis, -1)
    blocks = v.reshape(v.shape[:-1] + (-1, 32))
    amax = np.abs(blocks).max(-1, keepdims=True)
    byte = np.maximum(np.where(amax > 0, np.frexp(amax)[1] - 1 + 127, 0) - down, 1)
    scale = np.exp2(byte - 127.0)
    codes = (blocks / scale).astype(np.float32).astype(dtype).astype(np.float64)
    return np.moveaxis((codes * scale).reshape(v.shape), -1, axis)


WIDE = False


def mx_kscale(k):
    if not WIDE:
        return np.ones(k)
    levels = np.array([10, -10, 5, -5, 0])
    a = np.random.permutation(np.resize(levels, k // 512 * 4)).reshape(k // 512, 4)
    idx = np.arange(k)
    return np.exp2(a[idx // 512, idx % 128 // 32])


BF16 = ml_dtypes.bfloat16


def bf(x):
    return np.asarray(x, np.float32).astype(BF16)


def f64(x):
    return np.asarray(x).astype(np.float64)


E2M1 = np.array([0.0, 0.5, 1.0, 1.5, 2.0, 3.0, 4.0, 6.0, -0.0, -0.5, -1.0, -1.5, -2.0, -3.0, -4.0, -6.0])


def pack_weight(w, fmt):
    k, n = w.shape
    w = f64(bf(w)).reshape(k // 32, 32, n)
    amax = np.abs(w).max(1)
    if fmt == "e4m3":
        byte = np.frexp(amax)[1] - 1 + 127 - 7
    else:
        mant, ex = np.frexp(amax / 6.0)
        byte = np.where(mant > 0.5, ex, ex - 1) + 127
    byte = np.clip(np.where(amax > 0, byte, 1), 1, 254)
    scaled = (w * np.exp2(127.0 - byte)[:, None, :]).reshape(k, n).astype(np.float32)
    by_word = np.ascontiguousarray(scaled.reshape(k // 512, 128, 4, n).transpose(0, 1, 3, 2))
    if fmt == "e4m3":
        words = by_word.astype(ml_dtypes.float8_e4m3fn).view(np.uint8)
    else:
        c = by_word.astype(ml_dtypes.float4_e2m1fn).view(np.uint8) & 0xF
        words = c[..., 0::2] | (c[..., 1::2] << 4)
    return np.ascontiguousarray(words), np.ascontiguousarray(byte.astype(np.uint8).reshape(k // 512, 16, n))


def unpack_weight(words, scales, fmt):
    g, p, n, _ = words.shape
    if fmt == "e4m3":
        vals = np.ascontiguousarray(words).view(ml_dtypes.float8_e4m3fn).astype(np.float64)
    else:
        nib = np.empty((g, p, n, 4), np.uint8)
        nib[..., 0::2] = words & 0xF
        nib[..., 1::2] = words >> 4
        vals = E2M1[nib]
    vals = vals * np.repeat(np.exp2(scales.astype(np.float64) - 127.0), 8, axis=1)[..., None]
    return vals.transpose(0, 1, 3, 2).reshape(g * 512, n)

def pack4(w):
    words, scales = pack_weight(w, "e2m1")
    return words.reshape(words.shape[0], 128, -1), scales


def unpack4(words, scales):
    return unpack_weight(words.reshape(words.shape[0], 128, -1, 2), scales, "e2m1")


B, T, C, E, DV, R, G, BLK = 4, 1024, 512, 1024, 1024, 16, 16, 512
BASE = 1e4


def rope(x):
    inv_freq = 1.0 / (BASE ** (f64(np.arange(0, R, 2)) / R))
    ang = f64(np.arange(T))[:, None] * inv_freq[None, :]
    ang = np.repeat(ang, 2, axis=-1)
    cos, sin = np.cos(ang), np.sin(ang)
    xl, xr = x[..., :R], x[..., R:]
    p = xl.reshape(xl.shape[:-1] + (R // 2, 2))
    rot = np.stack((-p[..., 1], p[..., 0]), axis=-1).reshape(xl.shape)
    return np.concatenate([xl * cos + rot * sin, xr], axis=-1)


def setup_inputs():
    s = mx_kscale(C)
    Q_in = bf(np.random.standard_normal((B, T, C)) * s)
    wq_words, wq_scales = pack4(np.random.standard_normal((C, E)) * 0.25 / np.sqrt(C) / s[:, None])
    wk_words, wk_scales = pack4(np.random.standard_normal((C, E)) * 0.25 / np.sqrt(C) / s[:, None])
    return {"Q_in": Q_in,
            "W_Q_words": wq_words, "W_Q_scales": wq_scales,
            "W_K_words": wk_words, "W_K_scales": wk_scales}


def reference(Q_in, W_Q_words, W_Q_scales, W_K_words, W_K_scales):
    xq = mxq(f64(Q_in), 2, "e4m3")
    q = rope(xq @ unpack4(W_Q_words, W_Q_scales))
    k = rope(xq @ unpack4(W_K_words, W_K_scales))
    return q, k

@@ -1,0 +1,204 @@
+import math
+from contextlib import ExitStack
+
+import concourse.mybir as mybir
+from concourse.masks import make_identity
+
+F32 = mybir.dt.float32
+BF16 = mybir.dt.bfloat16
+I32 = mybir.dt.int32
+U32 = mybir.dt.uint32
+U8 = mybir.dt.uint8
+FP8X4 = mybir.dt.float8_e4m3fn_x4
+FP4X4 = mybir.dt.float4_e2m1fn_x4
+ALU = mybir.AluOpType
+SIN = mybir.ActivationFunctionType.Sin
+
+B, T, C, E = 4, 1024, 512, 1024
+ROPE_CHANNELS = 16
+ROPE_PAIRS = ROPE_CHANNELS // 2
+ROPE_BASE = 1e4
+
+P = 128
+PACK = 4
+N_PASS = 512
+ROWS = T // P
+TILES_PER_STORE = 4
+TILES_PER_PAIR = 2
+OUT_BUFS = 8
+
+assert C == P * PACK
+
+FLOPS = 2 * B * T * C * 2 * E
+
+TWO_PI_HI = 6.28125
+TWO_PI_LO = 2.0 * math.pi - TWO_PI_HI
+ROUND_MAGIC = 1.5 * 2.0**23
+
+
+def build_rope_tables(nc, pool):
+    shape = [P, ROWS, ROPE_PAIRS]
+    position_int = pool.tile([P, ROWS], I32)
+    nc.gpsimd.iota(position_int[:], pattern=[[1, ROWS]], base=0, channel_multiplier=ROWS)
+    position = pool.tile([P, ROWS], F32)
+    nc.vector.tensor_copy(out=position[:], in_=position_int[:])
+
+    angle = pool.tile(shape, F32)
+    for i in range(ROPE_PAIRS):
+        inv_freq = 1.0 / (ROPE_BASE ** (2.0 * i / ROPE_CHANNELS))
+        nc.vector.tensor_scalar_mul(out=angle[:, :, i], in0=position[:], scalar1=inv_freq)
+
+    turns = pool.tile(shape, F32)
+    nc.vector.tensor_scalar(
+        out=turns[:], in0=angle[:], scalar1=1.0 / (2.0 * math.pi), scalar2=ROUND_MAGIC, op0=ALU.mult, op1=ALU.add
+    )
+    nc.vector.tensor_scalar_sub(out=turns[:], in0=turns[:], scalar1=ROUND_MAGIC)
+    partly_reduced = pool.tile(shape, F32)
+    nc.vector.scalar_tensor_tensor(
+        out=partly_reduced[:], in0=turns[:], scalar=-TWO_PI_HI, in1=angle[:], op0=ALU.mult, op1=ALU.add
+    )
+    reduced = pool.tile(shape, F32)
+    nc.vector.scalar_tensor_tensor(
+        out=reduced[:], in0=turns[:], scalar=-TWO_PI_LO, in1=partly_reduced[:], op0=ALU.mult, op1=ALU.add
+    )
+
+    sin_half = pool.tile(shape, F32)
+    nc.scalar.activation(out=sin_half[:], in_=reduced[:], func=SIN, scale=0.5)
+    minus_abs = pool.tile(shape, F32)
+    nc.vector.scalar_tensor_tensor(
+        out=minus_abs[:], in0=reduced[:], scalar=-1.0, in1=reduced[:], op0=ALU.mult, op1=ALU.min
+    )
+    cos_half_angle = pool.tile(shape, F32)
+    nc.vector.tensor_scalar(
+        out=cos_half_angle[:], in0=minus_abs[:], scalar1=0.5, scalar2=0.5 * math.pi, op0=ALU.mult, op1=ALU.add
+    )
+    cos_half = pool.tile(shape, F32)
+    nc.scalar.activation(out=cos_half[:], in_=cos_half_angle[:], func=SIN)
+
+    sin = pool.tile(shape, F32)
+    nc.vector.scalar_tensor_tensor(
+        out=sin[:], in0=sin_half[:], scalar=2.0, in1=cos_half[:], op0=ALU.mult, op1=ALU.mult
+    )
+    minus_sin = pool.tile(shape, F32)
+    nc.vector.scalar_tensor_tensor(
+        out=minus_sin[:], in0=sin_half[:], scalar=-2.0, in1=cos_half[:], op0=ALU.mult, op1=ALU.mult
+    )
+    cos = pool.tile(shape, F32)
+    nc.vector.scalar_tensor_tensor(
+        out=cos[:], in0=sin_half[:], scalar=-2.0, in1=sin_half[:], op0=ALU.mult, op1=ALU.mult
+    )
+    nc.vector.tensor_scalar_add(out=cos[:], in0=cos[:], scalar1=1.0)
+    return cos, sin, minus_sin
+
+
+def tile_wqkv_pa_t_kernel(tc, Q_in, W_Q_words, W_Q_scales, W_K_words, W_K_scales, out_0, out_1):
+    nc = tc.nc
+    stores_per_batch = ROWS // TILES_PER_STORE
+    groups = [(b, s * TILES_PER_STORE) for b in range(B) for s in range(stores_per_batch)]
+    tokens_view = Q_in.rearrange("b (p j) c -> b p j c", j=ROWS)
+    out_views = [out.rearrange("b (p j) e -> b p j e", j=ROWS) for out in (out_0, out_1)]
+
+    with ExitStack() as ctx:
+        const_pool = ctx.enter_context(tc.tile_pool(name="const", bufs=1))
+        weight_pool = ctx.enter_context(tc.tile_pool(name="weight", bufs=2))
+        token_pool = ctx.enter_context(tc.tile_pool(name="token", bufs=len(groups)))
+        grouped_pool = ctx.enter_context(tc.tile_pool(name="grouped", bufs=4))
+        code_pool = ctx.enter_context(tc.tile_pool(name="code", bufs=6))
+        rope_pool = ctx.enter_context(tc.tile_pool(name="rope", bufs=4))
+        out_pool = ctx.enter_context(tc.tile_pool(name="out", bufs=OUT_BUFS))
+        transposed_pool = ctx.enter_context(tc.psum_pool(name="transposed", bufs=2))
+        product_pool = ctx.enter_context(tc.psum_pool(name="product", bufs=6))
+
+        def load_tokens(group):
+            b, first_row = group
+            tokens = token_pool.tile([P, TILES_PER_STORE, C], BF16)
+            nc.sync.dma_start(out=tokens[:], in_=tokens_view[b, :, first_row : first_row + TILES_PER_STORE, :])
+            return tokens
+
+        def load_weight(words_dram, scales_dram):
+            words = weight_pool.tile([P, 2 * E], U8, align_bytes=64)
+            nc.sync.dma_start(out=words[:].bitcast(I32), in_=words_dram[0].bitcast(I32))
+            plane = weight_pool.tile([P, E], U8, align_bytes=64)
+            nc.vector.memset(plane[:].bitcast(I32), 0)
+            for quadrant in range(4):
+                nc.sync.dma_start(
+                    out=plane[32 * quadrant : 32 * quadrant + 4, :].bitcast(I32),
+                    in_=scales_dram[0, 4 * quadrant : 4 * quadrant + 4, :].bitcast(I32),
+                )
+            return words, plane
+
+        def quantise_pair(tokens, first_tile):
+            words = tokens[:].bitcast(F32)
+            transposed = transposed_pool.tile([P, TILES_PER_PAIR, 2, P], F32)
+            for s in range(TILES_PER_PAIR):
+                for u in range(2):
+                    nc.tensor.transpose(transposed[:, s, u, :], words[:, first_tile + s, u : C // 2 : 2], identity[:])
+            grouped = grouped_pool.tile([P, TILES_PER_PAIR * P * PACK], BF16, align_bytes=64)
+            nc.scalar.copy(
+                out=grouped[:].bitcast(F32).rearrange("p (s m u) -> p s m u", s=TILES_PER_PAIR, u=2),
+                in_=transposed[:].rearrange("p s u m -> p s m u"),
+            )
+            codes = code_pool.tile([P, TILES_PER_PAIR * P], U32, align_bytes=64)
+            scales = code_pool.tile([P, TILES_PER_PAIR * P], U8, align_bytes=64)
+            nc.vector.quantize_mx(out=codes[:].bitcast(FP8X4), scales=scales[:], in_=grouped[:])
+            return codes, scales
+
+        def quantise_group(tokens):
+            return [quantise_pair(tokens, first_tile) for first_tile in range(0, TILES_PER_STORE, TILES_PER_PAIR)]
+
+        def rope(result, first_row):
+            rows = slice(first_row, first_row + TILES_PER_STORE)
+            head = result[:, :, 0:ROPE_CHANNELS].rearrange("p j (i e) -> p j i e", e=2)
+            straight = rope_pool.tile([P, TILES_PER_STORE, ROPE_PAIRS, 2], F32)
+            nc.vector.tensor_mul(
+                out=straight[:],
+                in0=head,
+                in1=cos[:, rows, :].unsqueeze(3).to_broadcast([P, TILES_PER_STORE, ROPE_PAIRS, 2]),
+            )
+            crossed = rope_pool.tile([P, 2, TILES_PER_STORE, ROPE_PAIRS], F32)
+            nc.vector.tensor_mul(out=crossed[:, 0], in0=head[:, :, :, 1], in1=minus_sin[:, rows, :])
+            nc.vector.tensor_mul(out=crossed[:, 1], in0=head[:, :, :, 0], in1=sin[:, rows, :])
+            nc.vector.tensor_add(out=head, in0=straight[:], in1=crossed[:].rearrange("p e j i -> p j i e"))
+
+        def project(group, quantised, which):
+            b, first_row = group
+            words, plane = weights[which]
+            result = out_pool.tile([P, TILES_PER_STORE, E], F32)
+            for j in range(TILES_PER_STORE):
+                codes, scales = quantised[j // TILES_PER_PAIR]
+                token_cols = slice((j % TILES_PER_PAIR) * P, (j % TILES_PER_PAIR + 1) * P)
+                for h in range(E // N_PASS):
+                    product = product_pool.tile([P, N_PASS], F32)
+                    nc.tensor.matmul_mx(
+                        out=product[:],
+                        lhsT=codes[:, token_cols].bitcast(FP8X4),
+                        lhsT_scale=scales[:, token_cols],
+                        rhs=words[:, 2 * N_PASS * h : 2 * N_PASS * (h + 1)].bitcast(FP4X4),
+                        rhs_scale=plane[:, N_PASS * h : N_PASS * (h + 1)],
+                        start=True,
+                        stop=True,
+                    )
+                    copy_out = nc.vector.tensor_copy if h == 0 else nc.scalar.copy
+                    copy_out(out=result[:, j, N_PASS * h : N_PASS * (h + 1)], in_=product[:])
+            rope(result, first_row)
+            nc.sync.dma_start(
+                out=out_views[which][b, :, first_row : first_row + TILES_PER_STORE, :], in_=result[:]
+            )
+
+        tokens_of = [load_tokens(groups[0])]
+        weights = [load_weight(W_Q_words, W_Q_scales)]
+        tokens_of.append(load_tokens(groups[1]))
+        weights.append(load_weight(W_K_words, W_K_scales))
+        tokens_of.extend(load_tokens(group) for group in groups[2:])
+
+        identity = const_pool.tile([P, P], F32)
+        make_identity(nc, identity[:])
+        cos, sin, minus_sin = build_rope_tables(nc, const_pool)
+
+        quantised_next = quantise_group(tokens_of[0])
+        for g, group in enumerate(groups):
+            quantised = quantised_next
+            project(group, quantised, 0)
+            if g + 1 < len(groups):
+                quantised_next = quantise_group(tokens_of[g + 1])
+            project(group, quantised, 1)

@@ -101,19 +101,18 @@ def tile_wqkv_pa_t_kernel(tc, Q_in, W_Q_words, W_Q_scales, W_K_words, W_K_scales
     with ExitStack() as ctx:
         const_pool = ctx.enter_context(tc.tile_pool(name="const", bufs=1))
         weight_pool = ctx.enter_context(tc.tile_pool(name="weight", bufs=2))
-        token_pool = ctx.enter_context(tc.tile_pool(name="token", bufs=len(groups)))
+        token_pool = ctx.enter_context(tc.tile_pool(name="token", bufs=B))
         grouped_pool = ctx.enter_context(tc.tile_pool(name="grouped", bufs=4))
         code_pool = ctx.enter_context(tc.tile_pool(name="code", bufs=6))
         rope_pool = ctx.enter_context(tc.tile_pool(name="rope", bufs=4))
         out_pool = ctx.enter_context(tc.tile_pool(name="out", bufs=OUT_BUFS))
         transposed_pool = ctx.enter_context(tc.psum_pool(name="transposed", bufs=2))
         product_pool = ctx.enter_context(tc.psum_pool(name="product", bufs=6))
+        ctx.enter_context(tc.manual_schedule())
 
-        def load_tokens(group):
-            b, first_row = group
-            tokens = token_pool.tile([P, TILES_PER_STORE, C], BF16)
-            nc.sync.dma_start(out=tokens[:], in_=tokens_view[b, :, first_row : first_row + TILES_PER_STORE, :])
-            return tokens
+        def load_tokens(b, first_row, n_rows):
+            rows = slice(first_row, first_row + n_rows)
+            nc.sync.dma_start(out=tokens_of[b][:, rows, :], in_=tokens_view[b, :, rows, :])
 
         def load_weight(words_dram, scales_dram):
             words = weight_pool.tile([P, 2 * E], U8, align_bytes=64)
@@ -127,12 +126,12 @@ def tile_wqkv_pa_t_kernel(tc, Q_in, W_Q_words, W_Q_scales, W_K_words, W_K_scales
                 )
             return words, plane
 
-        def quantise_pair(tokens, first_tile):
-            words = tokens[:].bitcast(F32)
+        def quantise_pair(b, first_row):
+            words = tokens_of[b][:].bitcast(F32)
             transposed = transposed_pool.tile([P, TILES_PER_PAIR, 2, P], F32)
             for s in range(TILES_PER_PAIR):
                 for u in range(2):
-                    nc.tensor.transpose(transposed[:, s, u, :], words[:, first_tile + s, u : C // 2 : 2], identity[:])
+                    nc.tensor.transpose(transposed[:, s, u, :], words[:, first_row + s, u : C // 2 : 2], identity[:])
             grouped = grouped_pool.tile([P, TILES_PER_PAIR * P * PACK], BF16, align_bytes=64)
             nc.scalar.copy(
                 out=grouped[:].bitcast(F32).rearrange("p (s m u) -> p s m u", s=TILES_PER_PAIR, u=2),
@@ -143,8 +142,9 @@ def tile_wqkv_pa_t_kernel(tc, Q_in, W_Q_words, W_Q_scales, W_K_words, W_K_scales
             nc.vector.quantize_mx(out=codes[:].bitcast(FP8X4), scales=scales[:], in_=grouped[:])
             return codes, scales
 
-        def quantise_group(tokens):
-            return [quantise_pair(tokens, first_tile) for first_tile in range(0, TILES_PER_STORE, TILES_PER_PAIR)]
+        def quantise_group(group):
+            b, first_row = group
+            return [quantise_pair(b, first_row + s) for s in range(0, TILES_PER_STORE, TILES_PER_PAIR)]
 
         def rope(result, first_row):
             rows = slice(first_row, first_row + TILES_PER_STORE)
@@ -185,20 +185,27 @@ def tile_wqkv_pa_t_kernel(tc, Q_in, W_Q_words, W_Q_scales, W_K_words, W_K_scales
                 out=out_views[which][b, :, first_row : first_row + TILES_PER_STORE, :], in_=result[:]
             )
 
-        tokens_of = [load_tokens(groups[0])]
+        tokens_of = []
+        for b in range(B):
+            tokens = token_pool.tile([P, ROWS, C], BF16)
+            tokens_of.append(tokens)
+
+        load_tokens(0, 0, TILES_PER_STORE)
         weights = [load_weight(W_Q_words, W_Q_scales)]
-        tokens_of.append(load_tokens(groups[1]))
+        load_tokens(0, TILES_PER_STORE, ROWS - TILES_PER_STORE)
+        load_tokens(1, 0, ROWS)
         weights.append(load_weight(W_K_words, W_K_scales))
-        tokens_of.extend(load_tokens(group) for group in groups[2:])
+        for b in range(2, B):
+            load_tokens(b, 0, ROWS)
 
         identity = const_pool.tile([P, P], F32)
         make_identity(nc, identity[:])
         cos, sin, minus_sin = build_rope_tables(nc, const_pool)
 
-        quantised_next = quantise_group(tokens_of[0])
+        quantised_next = quantise_group(groups[0])
         for g, group in enumerate(groups):
             quantised = quantised_next
             project(group, quantised, 0)
             if g + 1 < len(groups):
-                quantised_next = quantise_group(tokens_of[g + 1])
+                quantised_next = quantise_group(groups[g + 1])
             project(group, quantised, 1)

@@ -119,10 +119,10 @@ def tile_wqkv_pa_t_kernel(tc, Q_in, W_Q_words, W_Q_scales, W_K_words, W_K_scales
             nc.sync.dma_start(out=words[:].bitcast(I32), in_=words_dram[0].bitcast(I32))
             plane = weight_pool.tile([P, E], U8, align_bytes=64)
             nc.vector.memset(plane[:].bitcast(I32), 0)
-            for quadrant in range(4):
+            for r in range(4):
                 nc.sync.dma_start(
-                    out=plane[32 * quadrant : 32 * quadrant + 4, :].bitcast(I32),
-                    in_=scales_dram[0, 4 * quadrant : 4 * quadrant + 4, :].bitcast(I32),
+                    out=plane[r : P : 32, :].bitcast(I32),
+                    in_=scales_dram[0, r : 16 : 4, :].bitcast(I32),
                 )
             return words, plane
 

@@ -25,6 +25,7 @@ N_PASS = 512
 ROWS = T // P
 TILES_PER_STORE = 4
 TILES_PER_PAIR = 2
+DMA_ALIGN = 256
 OUT_BUFS = 8
 
 assert C == P * PACK
@@ -115,9 +116,9 @@ def tile_wqkv_pa_t_kernel(tc, Q_in, W_Q_words, W_Q_scales, W_K_words, W_K_scales
             nc.sync.dma_start(out=tokens_of[b][:, rows, :], in_=tokens_view[b, :, rows, :])
 
         def load_weight(words_dram, scales_dram):
-            words = weight_pool.tile([P, 2 * E], U8, align_bytes=64)
+            words = weight_pool.tile([P, 2 * E], U8, align_bytes=DMA_ALIGN)
             nc.sync.dma_start(out=words[:].bitcast(I32), in_=words_dram[0].bitcast(I32))
-            plane = weight_pool.tile([P, E], U8, align_bytes=64)
+            plane = weight_pool.tile([P, E], U8, align_bytes=DMA_ALIGN)
             nc.vector.memset(plane[:].bitcast(I32), 0)
             for r in range(4):
                 nc.sync.dma_start(
@@ -163,7 +164,7 @@ def tile_wqkv_pa_t_kernel(tc, Q_in, W_Q_words, W_Q_scales, W_K_words, W_K_scales
         def project(group, quantised, which):
             b, first_row = group
             words, plane = weights[which]
-            result = out_pool.tile([P, TILES_PER_STORE, E], F32)
+            result = out_pool.tile([P, TILES_PER_STORE, E], F32, align_bytes=DMA_ALIGN)
             for j in range(TILES_PER_STORE):
                 codes, scales = quantised[j // TILES_PER_PAIR]
                 token_cols = slice((j % TILES_PER_PAIR) * P, (j % TILES_PER_PAIR + 1) * P)
@@ -187,7 +188,7 @@ def tile_wqkv_pa_t_kernel(tc, Q_in, W_Q_words, W_Q_scales, W_K_words, W_K_scales
 
         tokens_of = []
         for b in range(B):
-            tokens = token_pool.tile([P, ROWS, C], BF16)
+            tokens = token_pool.tile([P, ROWS, C], BF16, align_bytes=DMA_ALIGN)
             tokens_of.append(tokens)
 
         load_tokens(0, 0, TILES_PER_STORE)

@@ -148,20 +148,21 @@ def tile_wqkv_pa_t_kernel(tc, Q_in, W_Q_words, W_Q_scales, W_K_words, W_K_scales
             return [quantise_pair(b, first_row + s) for s in range(0, TILES_PER_STORE, TILES_PER_PAIR)]
 
         def rope(result, first_row):
-            rows = slice(first_row, first_row + TILES_PER_STORE)
+            n_tiles = result.shape[1]
+            rows = slice(first_row, first_row + n_tiles)
             head = result[:, :, 0:ROPE_CHANNELS].rearrange("p j (i e) -> p j i e", e=2)
-            straight = rope_pool.tile([P, TILES_PER_STORE, ROPE_PAIRS, 2], F32)
+            straight = rope_pool.tile([P, n_tiles, ROPE_PAIRS, 2], F32)
             nc.vector.tensor_mul(
                 out=straight[:],
                 in0=head,
-                in1=cos[:, rows, :].unsqueeze(3).to_broadcast([P, TILES_PER_STORE, ROPE_PAIRS, 2]),
+                in1=cos[:, rows, :].unsqueeze(3).to_broadcast([P, n_tiles, ROPE_PAIRS, 2]),
             )
-            crossed = rope_pool.tile([P, 2, TILES_PER_STORE, ROPE_PAIRS], F32)
+            crossed = rope_pool.tile([P, 2, n_tiles, ROPE_PAIRS], F32)
             nc.vector.tensor_mul(out=crossed[:, 0], in0=head[:, :, :, 1], in1=minus_sin[:, rows, :])
             nc.vector.tensor_mul(out=crossed[:, 1], in0=head[:, :, :, 0], in1=sin[:, rows, :])
             nc.vector.tensor_add(out=head, in0=straight[:], in1=crossed[:].rearrange("p e j i -> p j i e"))
 
-        def project(group, quantised, which):
+        def project(group, quantised, which, tiles_per_dma=TILES_PER_STORE):
             b, first_row = group
             words, plane = weights[which]
             result = out_pool.tile([P, TILES_PER_STORE, E], F32, align_bytes=DMA_ALIGN)
@@ -181,10 +182,13 @@ def tile_wqkv_pa_t_kernel(tc, Q_in, W_Q_words, W_Q_scales, W_K_words, W_K_scales
                     )
                     copy_out = nc.vector.tensor_copy if h == 0 else nc.scalar.copy
                     copy_out(out=result[:, j, N_PASS * h : N_PASS * (h + 1)], in_=product[:])
-            rope(result, first_row)
-            nc.sync.dma_start(
-                out=out_views[which][b, :, first_row : first_row + TILES_PER_STORE, :], in_=result[:]
-            )
+                if (j + 1) % tiles_per_dma == 0:
+                    done = slice(j + 1 - tiles_per_dma, j + 1)
+                    piece_row = first_row + done.start
+                    rope(result[:, done, :], piece_row)
+                    nc.sync.dma_start(
+                        out=out_views[which][b, :, piece_row : piece_row + tiles_per_dma, :], in_=result[:, done, :]
+                    )
 
         tokens_of = []
         for b in range(B):
@@ -206,7 +210,7 @@ def tile_wqkv_pa_t_kernel(tc, Q_in, W_Q_words, W_Q_scales, W_K_words, W_K_scales
         quantised_next = quantise_group(groups[0])
         for g, group in enumerate(groups):
             quantised = quantised_next
-            project(group, quantised, 0)
+            project(group, quantised, 0, TILES_PER_PAIR if g == 0 else TILES_PER_STORE)
             if g + 1 < len(groups):
                 quantised_next = quantise_group(groups[g + 1])
             project(group, quantised, 1)

@@ -25,6 +25,8 @@ N_PASS = 512
 ROWS = T // P
 TILES_PER_STORE = 4
 TILES_PER_PAIR = 2
+WARM_UP_AT_START = 6
+WARM_UP_BEFORE_PRODUCTS = 2
 DMA_ALIGN = 256
 OUT_BUFS = 8
 
@@ -147,6 +149,11 @@ def tile_wqkv_pa_t_kernel(tc, Q_in, W_Q_words, W_Q_scales, W_K_words, W_K_scales
             b, first_row = group
             return [quantise_pair(b, first_row + s) for s in range(0, TILES_PER_STORE, TILES_PER_PAIR)]
 
+        def warm_up(n_matmuls):
+            unused = product_pool.tile([P, N_PASS], F32, tag="product")
+            for i in range(n_matmuls):
+                nc.tensor.matmul(unused[:], lhsT=zeros[:, 0:P], rhs=zeros[:], start=True, stop=True)
+
         def rope(result, first_row):
             n_tiles = result.shape[1]
             rows = slice(first_row, first_row + n_tiles)
@@ -197,6 +204,8 @@ def tile_wqkv_pa_t_kernel(tc, Q_in, W_Q_words, W_Q_scales, W_K_words, W_K_scales
 
         load_tokens(0, 0, TILES_PER_STORE)
         weights = [load_weight(W_Q_words, W_Q_scales)]
+        zeros = const_pool.tile([P, N_PASS], BF16)
+        nc.vector.memset(zeros[:], 0.0)
         load_tokens(0, TILES_PER_STORE, ROWS - TILES_PER_STORE)
         load_tokens(1, 0, ROWS)
         weights.append(load_weight(W_K_words, W_K_scales))
@@ -207,7 +216,9 @@ def tile_wqkv_pa_t_kernel(tc, Q_in, W_Q_words, W_Q_scales, W_K_words, W_K_scales
         make_identity(nc, identity[:])
         cos, sin, minus_sin = build_rope_tables(nc, const_pool)
 
+        warm_up(WARM_UP_AT_START)
         quantised_next = quantise_group(groups[0])
+        warm_up(WARM_UP_BEFORE_PRODUCTS)
         for g, group in enumerate(groups):
             quantised = quantised_next
             project(group, quantised, 0, TILES_PER_PAIR if g == 0 else TILES_PER_STORE)

@@ -22,13 +22,17 @@ ROPE_BASE = 1e4
 P = 128
 PACK = 4
 N_PASS = 512
-ROWS = T // P
-TILES_PER_STORE = 4
+SPAN = 2
+ROWS = SPAN * T // P
+TILE_ROWS = ROWS // 2
+SPANS = B // SPAN
+TILES_PER_GROUP = 4
+FIRST_COARSE_ENTRY = 1
 TILES_PER_PAIR = 2
-WARM_UP_AT_START = 6
+WARM_UP_AT_START = 5
 WARM_UP_BEFORE_PRODUCTS = 2
 DMA_ALIGN = 256
-OUT_BUFS = 8
+OUT_BUFS = 5
 
 assert C == P * PACK
 
@@ -39,10 +43,11 @@ TWO_PI_LO = 2.0 * math.pi - TWO_PI_HI
 ROUND_MAGIC = 1.5 * 2.0**23
 
 
-def build_rope_tables(nc, pool):
+def build_rope_angles(nc, pool):
     shape = [P, ROWS, ROPE_PAIRS]
     position_int = pool.tile([P, ROWS], I32)
     nc.gpsimd.iota(position_int[:], pattern=[[1, ROWS]], base=0, channel_multiplier=ROWS)
+    nc.vector.tensor_single_scalar(out=position_int[:], in_=position_int[:], scalar=T - 1, op=ALU.bitwise_and)
     position = pool.tile([P, ROWS], F32)
     nc.vector.tensor_copy(out=position[:], in_=position_int[:])
 
@@ -65,8 +70,6 @@ def build_rope_tables(nc, pool):
         out=reduced[:], in0=turns[:], scalar=-TWO_PI_LO, in1=partly_reduced[:], op0=ALU.mult, op1=ALU.add
     )
 
-    sin_half = pool.tile(shape, F32)
-    nc.scalar.activation(out=sin_half[:], in_=reduced[:], func=SIN, scale=0.5)
     minus_abs = pool.tile(shape, F32)
     nc.vector.scalar_tensor_tensor(
         out=minus_abs[:], in0=reduced[:], scalar=-1.0, in1=reduced[:], op0=ALU.mult, op1=ALU.min
@@ -75,6 +78,13 @@ def build_rope_tables(nc, pool):
     nc.vector.tensor_scalar(
         out=cos_half_angle[:], in0=minus_abs[:], scalar1=0.5, scalar2=0.5 * math.pi, op0=ALU.mult, op1=ALU.add
     )
+    return reduced, cos_half_angle
+
+
+def build_rope_tables(nc, pool, reduced, cos_half_angle):
+    shape = [P, ROWS, ROPE_PAIRS]
+    sin_half = pool.tile(shape, F32)
+    nc.scalar.activation(out=sin_half[:], in_=reduced[:], func=SIN, scale=0.5)
     cos_half = pool.tile(shape, F32)
     nc.scalar.activation(out=cos_half[:], in_=cos_half_angle[:], func=SIN)
 
@@ -96,17 +106,17 @@ def build_rope_tables(nc, pool):
 
 def tile_wqkv_pa_t_kernel(tc, Q_in, W_Q_words, W_Q_scales, W_K_words, W_K_scales, out_0, out_1):
     nc = tc.nc
-    stores_per_batch = ROWS // TILES_PER_STORE
-    groups = [(b, s * TILES_PER_STORE) for b in range(B) for s in range(stores_per_batch)]
-    tokens_view = Q_in.rearrange("b (p j) c -> b p j c", j=ROWS)
-    out_views = [out.rearrange("b (p j) e -> b p j e", j=ROWS) for out in (out_0, out_1)]
+    tiles = [(a, r) for a in range(SPANS) for r in range(0, ROWS, TILE_ROWS)]
+    groups = [[(a, r + s) for s in range(0, TILE_ROWS, TILES_PER_GROUP)] for a, r in tiles]
+    tokens_view = Q_in.rearrange("(a b) (q j) c -> a (b q) j c", b=SPAN, j=ROWS)
+    out_views = [out.rearrange("(a b) (q j) e -> a (b q) j e", b=SPAN, j=ROWS) for out in (out_0, out_1)]
 
     with ExitStack() as ctx:
         const_pool = ctx.enter_context(tc.tile_pool(name="const", bufs=1))
         weight_pool = ctx.enter_context(tc.tile_pool(name="weight", bufs=2))
-        token_pool = ctx.enter_context(tc.tile_pool(name="token", bufs=B))
+        token_pool = ctx.enter_context(tc.tile_pool(name="token", bufs=SPANS))
         grouped_pool = ctx.enter_context(tc.tile_pool(name="grouped", bufs=4))
-        code_pool = ctx.enter_context(tc.tile_pool(name="code", bufs=6))
+        code_pool = ctx.enter_context(tc.tile_pool(name="code", bufs=8))
         rope_pool = ctx.enter_context(tc.tile_pool(name="rope", bufs=4))
         out_pool = ctx.enter_context(tc.tile_pool(name="out", bufs=OUT_BUFS))
         transposed_pool = ctx.enter_context(tc.psum_pool(name="transposed", bufs=2))
@@ -147,34 +157,35 @@ def tile_wqkv_pa_t_kernel(tc, Q_in, W_Q_words, W_Q_scales, W_K_words, W_K_scales
 
         def quantise_group(group):
             b, first_row = group
-            return [quantise_pair(b, first_row + s) for s in range(0, TILES_PER_STORE, TILES_PER_PAIR)]
+            quantised[group] = [quantise_pair(b, first_row + s) for s in range(0, TILES_PER_GROUP, TILES_PER_PAIR)]
 
         def warm_up(n_matmuls):
             unused = product_pool.tile([P, N_PASS], F32, tag="product")
             for i in range(n_matmuls):
-                nc.tensor.matmul(unused[:], lhsT=zeros[:, 0:P], rhs=zeros[:], start=True, stop=True)
+                nc.tensor.matmul(unused[:], lhsT=zeros[:], rhs=zeros[:, 0:1].to_broadcast([P, N_PASS]), start=True, stop=True)
 
-        def rope(result, first_row):
+        def rope(result, first_row, urgent):
             n_tiles = result.shape[1]
+            engine = nc.vector if urgent else nc.gpsimd
             rows = slice(first_row, first_row + n_tiles)
             head = result[:, :, 0:ROPE_CHANNELS].rearrange("p j (i e) -> p j i e", e=2)
             straight = rope_pool.tile([P, n_tiles, ROPE_PAIRS, 2], F32)
-            nc.vector.tensor_mul(
+            engine.tensor_mul(
                 out=straight[:],
                 in0=head,
                 in1=cos[:, rows, :].unsqueeze(3).to_broadcast([P, n_tiles, ROPE_PAIRS, 2]),
             )
             crossed = rope_pool.tile([P, 2, n_tiles, ROPE_PAIRS], F32)
-            nc.vector.tensor_mul(out=crossed[:, 0], in0=head[:, :, :, 1], in1=minus_sin[:, rows, :])
-            nc.vector.tensor_mul(out=crossed[:, 1], in0=head[:, :, :, 0], in1=sin[:, rows, :])
-            nc.vector.tensor_add(out=head, in0=straight[:], in1=crossed[:].rearrange("p e j i -> p j i e"))
+            engine.tensor_mul(out=crossed[:, 0], in0=head[:, :, :, 1], in1=minus_sin[:, rows, :])
+            engine.tensor_mul(out=crossed[:, 1], in0=head[:, :, :, 0], in1=sin[:, rows, :])
+            engine.tensor_add(out=head, in0=straight[:], in1=crossed[:].rearrange("p e j i -> p j i e"))
 
-        def project(group, quantised, which, tiles_per_dma=TILES_PER_STORE):
-            b, first_row = group
+        def project(group, result, which, tiles_per_dma, urgent=False):
+            a, first_row = group
+            tile_start = first_row - first_row % TILE_ROWS
             words, plane = weights[which]
-            result = out_pool.tile([P, TILES_PER_STORE, E], F32, align_bytes=DMA_ALIGN)
-            for j in range(TILES_PER_STORE):
-                codes, scales = quantised[j // TILES_PER_PAIR]
+            for j in range(TILES_PER_GROUP):
+                codes, scales = quantised[group][j // TILES_PER_PAIR]
                 token_cols = slice((j % TILES_PER_PAIR) * P, (j % TILES_PER_PAIR + 1) * P)
                 for h in range(E // N_PASS):
                     product = product_pool.tile([P, N_PASS], F32)
@@ -188,40 +199,63 @@ def tile_wqkv_pa_t_kernel(tc, Q_in, W_Q_words, W_Q_scales, W_K_words, W_K_scales
                         stop=True,
                     )
                     copy_out = nc.vector.tensor_copy if h == 0 else nc.scalar.copy
-                    copy_out(out=result[:, j, N_PASS * h : N_PASS * (h + 1)], in_=product[:])
-                if (j + 1) % tiles_per_dma == 0:
-                    done = slice(j + 1 - tiles_per_dma, j + 1)
-                    piece_row = first_row + done.start
-                    rope(result[:, done, :], piece_row)
+                    copy_out(out=result[:, first_row - tile_start + j, N_PASS * h : N_PASS * (h + 1)], in_=product[:])
+                end = first_row - tile_start + j + 1
+                n_roped = min(tiles_per_dma, TILES_PER_GROUP)
+                if end % n_roped == 0:
+                    rope(result[:, end - n_roped : end, :], tile_start + end - n_roped, urgent)
+                if end % tiles_per_dma == 0:
+                    rows = slice(tile_start + end - tiles_per_dma, tile_start + end)
                     nc.sync.dma_start(
-                        out=out_views[which][b, :, piece_row : piece_row + tiles_per_dma, :], in_=result[:, done, :]
+                        out=out_views[which][a, :, rows, :], in_=result[:, end - tiles_per_dma : end, :]
                     )
 
+        quantised = {}
         tokens_of = []
-        for b in range(B):
+        for a in range(SPANS):
             tokens = token_pool.tile([P, ROWS, C], BF16, align_bytes=DMA_ALIGN)
             tokens_of.append(tokens)
 
-        load_tokens(0, 0, TILES_PER_STORE)
-        weights = [load_weight(W_Q_words, W_Q_scales)]
-        zeros = const_pool.tile([P, N_PASS], BF16)
+        zeros = const_pool.tile([P, P], BF16)
         nc.vector.memset(zeros[:], 0.0)
-        load_tokens(0, TILES_PER_STORE, ROWS - TILES_PER_STORE)
-        load_tokens(1, 0, ROWS)
+        unused_sine = const_pool.tile([P, 1], F32)
+        nc.scalar.activation(out=unused_sine[:], in_=zeros[:, 0:1], func=SIN)
+        load_tokens(0, 0, TILES_PER_GROUP)
+        weights = [load_weight(W_Q_words, W_Q_scales)]
+        load_tokens(0, TILES_PER_GROUP, ROWS - TILES_PER_GROUP)
         weights.append(load_weight(W_K_words, W_K_scales))
-        for b in range(2, B):
-            load_tokens(b, 0, ROWS)
+        for a in range(1, SPANS):
+            load_tokens(a, 0, ROWS)
 
         identity = const_pool.tile([P, P], F32)
         make_identity(nc, identity[:])
-        cos, sin, minus_sin = build_rope_tables(nc, const_pool)
+        reduced, cos_half_angle = build_rope_angles(nc, const_pool)
 
         warm_up(WARM_UP_AT_START)
-        quantised_next = quantise_group(groups[0])
+        quantise_group(groups[0][0])
+        cos, sin, minus_sin = build_rope_tables(nc, const_pool, reduced, cos_half_angle)
         warm_up(WARM_UP_BEFORE_PRODUCTS)
-        for g, group in enumerate(groups):
-            quantised = quantised_next
-            project(group, quantised, 0, TILES_PER_PAIR if g == 0 else TILES_PER_STORE)
-            if g + 1 < len(groups):
-                quantised_next = quantise_group(groups[g + 1])
-            project(group, quantised, 1)
+        for b in range(len(tiles)):
+            first, second = groups[b]
+            results = []
+            for which in range(2):
+                result = out_pool.tile([P, TILE_ROWS, E], F32, align_bytes=DMA_ALIGN)
+                results.append(result)
+            if b < FIRST_COARSE_ENTRY:
+                project(first, results[0], 0, TILES_PER_PAIR if b == 0 else TILES_PER_GROUP, urgent=b == 0)
+                quantise_group(second)
+                project(first, results[1], 1, TILES_PER_GROUP, urgent=b == 0)
+                project(second, results[0], 0, TILES_PER_GROUP)
+                quantise_group(groups[b + 1][0])
+                project(second, results[1], 1, TILES_PER_GROUP)
+                if b + 1 == FIRST_COARSE_ENTRY:
+                    quantise_group(groups[b + 1][1])
+            else:
+                project(first, results[0], 0, TILE_ROWS)
+                project(second, results[0], 0, TILE_ROWS, urgent=b == FIRST_COARSE_ENTRY)
+                if b + 1 < len(tiles):
+                    quantise_group(groups[b + 1][0])
+                project(first, results[1], 1, TILE_ROWS)
+                if b + 1 < len(tiles):
+                    quantise_group(groups[b + 1][1])
+                project(second, results[1], 1, TILE_ROWS)

@@ -31,6 +31,7 @@ FIRST_COARSE_ENTRY = 1
 TILES_PER_PAIR = 2
 WARM_UP_AT_START = 5
 WARM_UP_BEFORE_PRODUCTS = 2
+PACKET_ALIGN = 4096
 DMA_ALIGN = 256
 OUT_BUFS = 5
 
@@ -213,7 +214,7 @@ def tile_wqkv_pa_t_kernel(tc, Q_in, W_Q_words, W_Q_scales, W_K_words, W_K_scales
         quantised = {}
         tokens_of = []
         for a in range(SPANS):
-            tokens = token_pool.tile([P, ROWS, C], BF16, align_bytes=DMA_ALIGN)
+            tokens = token_pool.tile([P, ROWS, C], BF16, align_bytes=PACKET_ALIGN)
             tokens_of.append(tokens)
 
         zeros = const_pool.tile([P, P], BF16)
@@ -239,7 +240,7 @@ def tile_wqkv_pa_t_kernel(tc, Q_in, W_Q_words, W_Q_scales, W_K_words, W_K_scales
             first, second = groups[b]
             results = []
             for which in range(2):
-                result = out_pool.tile([P, TILE_ROWS, E], F32, align_bytes=DMA_ALIGN)
+                result = out_pool.tile([P, TILE_ROWS, E], F32, align_bytes=PACKET_ALIGN)
                 results.append(result)
             if b < FIRST_COARSE_ENTRY:
                 project(first, results[0], 0, TILES_PER_PAIR if b == 0 else TILES_PER_GROUP, urgent=b == 0)

@@ -243,7 +243,7 @@ def tile_wqkv_pa_t_kernel(tc, Q_in, W_Q_words, W_Q_scales, W_K_words, W_K_scales
                 result = out_pool.tile([P, TILE_ROWS, E], F32, align_bytes=PACKET_ALIGN)
                 results.append(result)
             if b < FIRST_COARSE_ENTRY:
-                project(first, results[0], 0, TILES_PER_PAIR if b == 0 else TILES_PER_GROUP, urgent=b == 0)
+                project(first, results[0], 0, TILES_PER_GROUP, urgent=b == 0)
                 quantise_group(second)
                 project(first, results[1], 1, TILES_PER_GROUP, urgent=b == 0)
                 project(second, results[0], 0, TILES_PER_GROUP)

import math
from contextlib import ExitStack

import concourse.mybir as mybir
from concourse.masks import make_identity

F32 = mybir.dt.float32
BF16 = mybir.dt.bfloat16
I32 = mybir.dt.int32
U32 = mybir.dt.uint32
U8 = mybir.dt.uint8
FP8X4 = mybir.dt.float8_e4m3fn_x4
FP4X4 = mybir.dt.float4_e2m1fn_x4
ALU = mybir.AluOpType
SIN = mybir.ActivationFunctionType.Sin

B, T, C, E = 4, 1024, 512, 1024
ROPE_CHANNELS = 16
ROPE_PAIRS = ROPE_CHANNELS // 2
ROPE_BASE = 1e4

P = 128
PACK = 4
N_PASS = 512
SPAN = 2
ROWS = SPAN * T // P
TILE_ROWS = ROWS // 2
SPANS = B // SPAN
TILES_PER_GROUP = 4
FIRST_COARSE_ENTRY = 1
TILES_PER_PAIR = 2
WARM_UP_AT_START = 5
WARM_UP_BEFORE_PRODUCTS = 2
PACKET_ALIGN = 4096
DMA_ALIGN = 256
OUT_BUFS = 5

assert C == P * PACK

FLOPS = 2 * B * T * C * 2 * E

TWO_PI_HI = 6.28125
TWO_PI_LO = 2.0 * math.pi - TWO_PI_HI
ROUND_MAGIC = 1.5 * 2.0**23


def build_rope_angles(nc, pool):
    shape = [P, ROWS, ROPE_PAIRS]
    position_int = pool.tile([P, ROWS], I32)
    nc.gpsimd.iota(position_int[:], pattern=[[1, ROWS]], base=0, channel_multiplier=ROWS)
    nc.vector.tensor_single_scalar(out=position_int[:], in_=position_int[:], scalar=T - 1, op=ALU.bitwise_and)
    position = pool.tile([P, ROWS], F32)
    nc.vector.tensor_copy(out=position[:], in_=position_int[:])

    angle = pool.tile(shape, F32)
    for i in range(ROPE_PAIRS):
        inv_freq = 1.0 / (ROPE_BASE ** (2.0 * i / ROPE_CHANNELS))
        nc.vector.tensor_scalar_mul(out=angle[:, :, i], in0=position[:], scalar1=inv_freq)

    turns = pool.tile(shape, F32)
    nc.vector.tensor_scalar(
        out=turns[:], in0=angle[:], scalar1=1.0 / (2.0 * math.pi), scalar2=ROUND_MAGIC, op0=ALU.mult, op1=ALU.add
    )
    nc.vector.tensor_scalar_sub(out=turns[:], in0=turns[:], scalar1=ROUND_MAGIC)
    partly_reduced = pool.tile(shape, F32)
    nc.vector.scalar_tensor_tensor(
        out=partly_reduced[:], in0=turns[:], scalar=-TWO_PI_HI, in1=angle[:], op0=ALU.mult, op1=ALU.add
    )
    reduced = pool.tile(shape, F32)
    nc.vector.scalar_tensor_tensor(
        out=reduced[:], in0=turns[:], scalar=-TWO_PI_LO, in1=partly_reduced[:], op0=ALU.mult, op1=ALU.add
    )

    minus_abs = pool.tile(shape, F32)
    nc.vector.scalar_tensor_tensor(
        out=minus_abs[:], in0=reduced[:], scalar=-1.0, in1=reduced[:], op0=ALU.mult, op1=ALU.min
    )
    cos_half_angle = pool.tile(shape, F32)
    nc.vector.tensor_scalar(
        out=cos_half_angle[:], in0=minus_abs[:], scalar1=0.5, scalar2=0.5 * math.pi, op0=ALU.mult, op1=ALU.add
    )
    return reduced, cos_half_angle


def build_rope_tables(nc, pool, reduced, cos_half_angle):
    shape = [P, ROWS, ROPE_PAIRS]
    sin_half = pool.tile(shape, F32)
    nc.scalar.activation(out=sin_half[:], in_=reduced[:], func=SIN, scale=0.5)
    cos_half = pool.tile(shape, F32)
    nc.scalar.activation(out=cos_half[:], in_=cos_half_angle[:], func=SIN)

    sin = pool.tile(shape, F32)
    nc.vector.scalar_tensor_tensor(
        out=sin[:], in0=sin_half[:], scalar=2.0, in1=cos_half[:], op0=ALU.mult, op1=ALU.mult
    )
    minus_sin = pool.tile(shape, F32)
    nc.vector.scalar_tensor_tensor(
        out=minus_sin[:], in0=sin_half[:], scalar=-2.0, in1=cos_half[:], op0=ALU.mult, op1=ALU.mult
    )
    cos = pool.tile(shape, F32)
    nc.vector.scalar_tensor_tensor(
        out=cos[:], in0=sin_half[:], scalar=-2.0, in1=sin_half[:], op0=ALU.mult, op1=ALU.mult
    )
    nc.vector.tensor_scalar_add(out=cos[:], in0=cos[:], scalar1=1.0)
    return cos, sin, minus_sin


def tile_wqkv_pa_t_kernel(tc, Q_in, W_Q_words, W_Q_scales, W_K_words, W_K_scales, out_0, out_1):
    nc = tc.nc
    tiles = [(a, r) for a in range(SPANS) for r in range(0, ROWS, TILE_ROWS)]
    groups = [[(a, r + s) for s in range(0, TILE_ROWS, TILES_PER_GROUP)] for a, r in tiles]
    tokens_view = Q_in.rearrange("(a b) (q j) c -> a (b q) j c", b=SPAN, j=ROWS)
    out_views = [out.rearrange("(a b) (q j) e -> a (b q) j e", b=SPAN, j=ROWS) for out in (out_0, out_1)]

    with ExitStack() as ctx:
        const_pool = ctx.enter_context(tc.tile_pool(name="const", bufs=1))
        weight_pool = ctx.enter_context(tc.tile_pool(name="weight", bufs=2))
        token_pool = ctx.enter_context(tc.tile_pool(name="token", bufs=SPANS))
        grouped_pool = ctx.enter_context(tc.tile_pool(name="grouped", bufs=4))
        code_pool = ctx.enter_context(tc.tile_pool(name="code", bufs=8))
        rope_pool = ctx.enter_context(tc.tile_pool(name="rope", bufs=4))
        out_pool = ctx.enter_context(tc.tile_pool(name="out", bufs=OUT_BUFS))
        transposed_pool = ctx.enter_context(tc.psum_pool(name="transposed", bufs=2))
        product_pool = ctx.enter_context(tc.psum_pool(name="product", bufs=6))
        ctx.enter_context(tc.manual_schedule())

        def load_tokens(b, first_row, n_rows):
            rows = slice(first_row, first_row + n_rows)
            nc.sync.dma_start(out=tokens_of[b][:, rows, :], in_=tokens_view[b, :, rows, :])

        def load_weight(words_dram, scales_dram):
            words = weight_pool.tile([P, 2 * E], U8, align_bytes=DMA_ALIGN)
            nc.sync.dma_start(out=words[:].bitcast(I32), in_=words_dram[0].bitcast(I32))
            plane = weight_pool.tile([P, E], U8, align_bytes=DMA_ALIGN)
            nc.vector.memset(plane[:].bitcast(I32), 0)
            for r in range(4):
                nc.sync.dma_start(
                    out=plane[r : P : 32, :].bitcast(I32),
                    in_=scales_dram[0, r : 16 : 4, :].bitcast(I32),
                )
            return words, plane

        def quantise_pair(b, first_row):
            words = tokens_of[b][:].bitcast(F32)
            transposed = transposed_pool.tile([P, TILES_PER_PAIR, 2, P], F32)
            for s in range(TILES_PER_PAIR):
                for u in range(2):
                    nc.tensor.transpose(transposed[:, s, u, :], words[:, first_row + s, u : C // 2 : 2], identity[:])
            grouped = grouped_pool.tile([P, TILES_PER_PAIR * P * PACK], BF16, align_bytes=64)
            nc.scalar.copy(
                out=grouped[:].bitcast(F32).rearrange("p (s m u) -> p s m u", s=TILES_PER_PAIR, u=2),
                in_=transposed[:].rearrange("p s u m -> p s m u"),
            )
            codes = code_pool.tile([P, TILES_PER_PAIR * P], U32, align_bytes=64)
            scales = code_pool.tile([P, TILES_PER_PAIR * P], U8, align_bytes=64)
            nc.vector.quantize_mx(out=codes[:].bitcast(FP8X4), scales=scales[:], in_=grouped[:])
            return codes, scales

        def quantise_group(group):
            b, first_row = group
            quantised[group] = [quantise_pair(b, first_row + s) for s in range(0, TILES_PER_GROUP, TILES_PER_PAIR)]

        def warm_up(n_matmuls):
            unused = product_pool.tile([P, N_PASS], F32, tag="product")
            for i in range(n_matmuls):
                nc.tensor.matmul(unused[:], lhsT=zeros[:], rhs=zeros[:, 0:1].to_broadcast([P, N_PASS]), start=True, stop=True)

        def rope(result, first_row, urgent):
            n_tiles = result.shape[1]
            engine = nc.vector if urgent else nc.gpsimd
            rows = slice(first_row, first_row + n_tiles)
            head = result[:, :, 0:ROPE_CHANNELS].rearrange("p j (i e) -> p j i e", e=2)
            straight = rope_pool.tile([P, n_tiles, ROPE_PAIRS, 2], F32)
            engine.tensor_mul(
                out=straight[:],
                in0=head,
                in1=cos[:, rows, :].unsqueeze(3).to_broadcast([P, n_tiles, ROPE_PAIRS, 2]),
            )
            crossed = rope_pool.tile([P, 2, n_tiles, ROPE_PAIRS], F32)
            engine.tensor_mul(out=crossed[:, 0], in0=head[:, :, :, 1], in1=minus_sin[:, rows, :])
            engine.tensor_mul(out=crossed[:, 1], in0=head[:, :, :, 0], in1=sin[:, rows, :])
            engine.tensor_add(out=head, in0=straight[:], in1=crossed[:].rearrange("p e j i -> p j i e"))

        def project(group, result, which, tiles_per_dma, urgent=False):
            a, first_row = group
            tile_start = first_row - first_row % TILE_ROWS
            words, plane = weights[which]
            for j in range(TILES_PER_GROUP):
                codes, scales = quantised[group][j // TILES_PER_PAIR]
                token_cols = slice((j % TILES_PER_PAIR) * P, (j % TILES_PER_PAIR + 1) * P)
                for h in range(E // N_PASS):
                    product = product_pool.tile([P, N_PASS], F32)
                    nc.tensor.matmul_mx(
                        out=product[:],
                        lhsT=codes[:, token_cols].bitcast(FP8X4),
                        lhsT_scale=scales[:, token_cols],
                        rhs=words[:, 2 * N_PASS * h : 2 * N_PASS * (h + 1)].bitcast(FP4X4),
                        rhs_scale=plane[:, N_PASS * h : N_PASS * (h + 1)],
                        start=True,
                        stop=True,
                    )
                    copy_out = nc.vector.tensor_copy if h == 0 else nc.scalar.copy
                    copy_out(out=result[:, first_row - tile_start + j, N_PASS * h : N_PASS * (h + 1)], in_=product[:])
                end = first_row - tile_start + j + 1
                n_roped = min(tiles_per_dma, TILES_PER_GROUP)
                if end % n_roped == 0:
                    rope(result[:, end - n_roped : end, :], tile_start + end - n_roped, urgent)
                if end % tiles_per_dma == 0:
                    rows = slice(tile_start + end - tiles_per_dma, tile_start + end)
                    nc.sync.dma_start(
                        out=out_views[which][a, :, rows, :], in_=result[:, end - tiles_per_dma : end, :]
                    )

        quantised = {}
        tokens_of = []
        for a in range(SPANS):
            tokens = token_pool.tile([P, ROWS, C], BF16, align_bytes=PACKET_ALIGN)
            tokens_of.append(tokens)

        zeros = const_pool.tile([P, P], BF16)
        nc.vector.memset(zeros[:], 0.0)
        unused_sine = const_pool.tile([P, 1], F32)
        nc.scalar.activation(out=unused_sine[:], in_=zeros[:, 0:1], func=SIN)
        load_tokens(0, 0, TILES_PER_GROUP)
        weights = [load_weight(W_Q_words, W_Q_scales)]
        load_tokens(0, TILES_PER_GROUP, ROWS - TILES_PER_GROUP)
        weights.append(load_weight(W_K_words, W_K_scales))
        for a in range(1, SPANS):
            load_tokens(a, 0, ROWS)

        identity = const_pool.tile([P, P], F32)
        make_identity(nc, identity[:])
        reduced, cos_half_angle = build_rope_angles(nc, const_pool)

        warm_up(WARM_UP_AT_START)
        quantise_group(groups[0][0])
        cos, sin, minus_sin = build_rope_tables(nc, const_pool, reduced, cos_half_angle)
        warm_up(WARM_UP_BEFORE_PRODUCTS)
        for b in range(len(tiles)):
            first, second = groups[b]
            results = []
            for which in range(2):
                result = out_pool.tile([P, TILE_ROWS, E], F32, align_bytes=PACKET_ALIGN)
                results.append(result)
            if b < FIRST_COARSE_ENTRY:
                project(first, results[0], 0, TILES_PER_GROUP, urgent=b == 0)
                quantise_group(second)
                project(first, results[1], 1, TILES_PER_GROUP, urgent=b == 0)
                project(second, results[0], 0, TILES_PER_GROUP)
                quantise_group(groups[b + 1][0])
                project(second, results[1], 1, TILES_PER_GROUP)
                if b + 1 == FIRST_COARSE_ENTRY:
                    quantise_group(groups[b + 1][1])
            else:
                project(first, results[0], 0, TILE_ROWS)
                project(second, results[0], 0, TILE_ROWS, urgent=b == FIRST_COARSE_ENTRY)
                if b + 1 < len(tiles):
                    quantise_group(groups[b + 1][0])
                project(first, results[1], 1, TILE_ROWS)
                if b + 1 < len(tiles):
                    quantise_group(groups[b + 1][1])
                project(second, results[1], 1, TILE_ROWS)
